import numpy as np
import ml_dtypes


def mxq(x, axis, fmt="e4m3"):
    dtype, down = {"e4m3": (ml_dtypes.float8_e4m3fn, 7), "e5m2": (ml_dtypes.float8_e5m2, 14)}[fmt]
    v = np.moveaxis(np.asarray(x, np.float32).astype(ml_dtypes.bfloat16).astype(np.float64), axis, -1)
    blocks = v.reshape(v.shape[:-1] + (-1, 32))
    amax = np.abs(blocks).max(-1, keepdims=True)
    byte = np.maximum(np.where(amax > 0, np.frexp(amax)[1] - 1 + 127, 0) - down, 1)
    scale = np.exp2(byte - 127.0)
    codes = (blocks / scale).astype(np.float32).astype(dtype).astype(np.float64)
    return np.moveaxis((codes * scale).reshape(v.shape), -1, axis)


WIDE = False


def mx_kscale(k):
    if not WIDE:
        return np.ones(k)
    levels = np.array([10, -10, 5, -5, 0])
    if k % 512:
        return np.exp2(np.random.permutation(np.resize(levels, k // 32))).repeat(32)
    a = np.empty((k // 512, 16))
    for p in range(k // 512):
        a[p, :8] = np.random.permutation(np.resize(levels, 8))
        for g in range(8):
            far = levels[np.abs(levels - a[p, g]) >= 10]
            a[p, g + 8] = far[np.random.randint(len(far))]
    return np.exp2(a.ravel()).repeat(32)


BF16 = ml_dtypes.bfloat16


def bf(x):
    return np.asarray(x, np.float32).astype(BF16)


def f64(x):
    return np.asarray(x).astype(np.float64)


B, T, C, H, KH, D = 4, 512, 4096, 32, 8, 128
HD = H * D


def sigmoid(v):
    return 1.0 / (1.0 + np.exp(-v))


def setup_inputs():
    s, t = mx_kscale(C), mx_kscale(HD)
    return {"x": bf(np.random.standard_normal((B, T, C)) * s),
            "y_attn": bf((np.random.standard_normal((B, T, HD)) * 0.3 * t).reshape(B, T, H, D)),
            "w_gate": bf(np.random.standard_normal((C, HD)) / np.sqrt(C) / s[:, None]),
            "w_proj": bf(np.random.standard_normal((HD, C)) * 3.0 / np.sqrt(HD) / t[:, None])}


def reference(x, y_attn, w_gate, w_proj):
    gate = sigmoid((mxq(f64(x), 2, "e4m3") @ mxq(f64(w_gate), 0, "e4m3")).reshape(B, T, H, D))
    y = f64(y_attn) * gate
    return mxq(y.reshape(B, T, HD), 2, "e4m3") @ mxq(f64(w_proj), 0, "e4m3")

@@ -1,0 +1,368 @@
+from contextlib import ExitStack
+
+import concourse.mybir as mybir
+from concourse.masks import make_identity
+
+FLOPS = 2 * 2 * 2048 * 4096 * 4096
+
+F32 = mybir.dt.float32
+BF16 = mybir.dt.bfloat16
+U32 = mybir.dt.uint32
+U8 = mybir.dt.uint8
+FP8X4 = mybir.dt.float8_e4m3fn_x4
+ACT = mybir.ActivationFunctionType
+ALU = mybir.AluOpType
+
+P = 128
+
+
+def tile_multiheadattention_pb_l_kernel(tc, x, y_attn, w_gate, w_proj, out):
+    nc = tc.nc
+    xf = x.rearrange("b t c -> (b t) c")
+    yf = y_attn.rearrange("b t h d -> (b t) (h d)")
+    of = out.rearrange("b t c -> (b t) c")
+
+    with ExitStack() as ctx:
+        sb = ctx.enter_context(tc.tile_pool(name="sb", bufs=1))
+        ps = ctx.enter_context(tc.psum_pool(name="ps", bufs=2))
+
+        ident = sb.tile([P, P], F32, name="ident", tag="ident")
+        make_identity(nc, ident[:])
+        warm_in = sb.tile([P, 8], F32, name="warm_in", tag="warm_in")
+        warm_out = sb.tile([P, 8], F32, name="warm_out", tag="warm_out")
+        nc.vector.memset(warm_in[:], 0.0)
+        nc.scalar.activation(out=warm_out[:], in_=warm_in[:], func=ACT.Sigmoid)
+
+        wraw = {}
+        wgrp = {}
+        wc = {}
+        ws = {}
+        xraw = {}
+        xbank = {}
+        xin = {}
+        xc = {}
+        xs = {}
+        yraw = {}
+        ysrt = {}
+        ybank = {}
+        sig = {}
+        hb = {}
+        hc = {}
+        hs = {}
+        counter = {"acc": 0}
+
+        def w_load(j):
+            if j >= 128:
+                return
+            c, q = divmod(j, 8)
+            src = w_gate if c < 8 else w_proj
+            col = (c % 8) * 512
+            t = sb.tile([P, 4, 512], BF16, name="wraw", tag="wraw", bufs=3)
+            nc.sync.dma_start(
+                out=t[:], in_=src[q * 512 : (q + 1) * 512, col : col + 512].rearrange("(p j) c -> p j c", j=4)
+            )
+            wraw[j] = t
+
+        def w_group(j):
+            if j >= 128:
+                return
+            g = sb.tile([P, 2048], BF16, name="wgrp", tag="wgrp", bufs=2, align_bytes=64)
+            r = wraw.pop(j)
+            if j < 64:
+                nc.vector.tensor_copy(
+                    out=g[:].rearrange("p (t m j) -> p t m j", t=4, j=4),
+                    in_=r[:].rearrange("p j (m t) -> p t m j", t=4),
+                )
+            else:
+                nc.vector.tensor_copy(
+                    out=g[:].rearrange("p (c j) -> p c j", j=4), in_=r[:].rearrange("p j c -> p c j")
+                )
+            wgrp[j] = g
+
+        def w_quant(j):
+            if j >= 128:
+                return
+            c, q = divmod(j, 8)
+            wc[j] = sb.tile([P, 512], U32, name="wc%d" % q, tag="wc%d" % q, bufs=2, align_bytes=64)
+            if q % 4 == 0:
+                ws[(c, q // 4)] = sb.tile(
+                    [P, 512], U8, name="ws%d" % (q // 4), tag="ws%d" % (q // 4), bufs=2, align_bytes=64
+                )
+            nc.vector.quantize_mx(
+                out=wc[j][:].bitcast(FP8X4), scales=ws[(c, q // 4)][4 * (q % 4) : P, :], in_=wgrp.pop(j)[:]
+            )
+
+        plan = {}
+        for c in range(16):
+            for q in range(8):
+                j = 8 * (c + 1) + q
+                if c == 0:
+                    kg = (4, 5, 7, 8, 10, 11, 13, 14)[q]
+                    kq = kg + 1
+                    plan[(0, kg, "g")] = j
+                    plan[(0, kq, "q")] = j
+                else:
+                    if q == 0:
+                        plan[(c - 1, 15, "g")] = j
+                    else:
+                        plan[(c, 2 * q - 1, "g")] = j
+                    plan[(c, 2 * q, "q")] = j
+
+        def w_background(c, k):
+            j = plan.get((c, k, "q"))
+            if j is not None:
+                w_quant(j)
+            j = plan.get((c, k, "g"))
+            if j is not None:
+                w_group(j)
+                w_load(j + 3)
+
+        def x_load(st):
+            if st >= 16:
+                return
+            tcx, gp = divmod(st, 4)
+            t = sb.tile([P, 4, 1024], BF16, name="xraw", tag="s8", bufs=8, align_bytes=64)
+            nc.sync.dma_start(
+                out=t[:],
+                in_=xf[tcx * 512 : (tcx + 1) * 512, gp * 1024 : (gp + 1) * 1024].rearrange("(i p) c -> p i c", p=P),
+            )
+            xraw[st] = t
+
+        def x_transpose(e):
+            words = xraw[e // 2][:].bitcast(F32)
+            base = (e % 2) * 256
+            b0 = ps.tile([P, 512], F32, name="xb", tag="xb", bufs=4)
+            b1 = ps.tile([P, 512], F32, name="xb", tag="xb", bufs=4)
+            xbank[e] = (b0, b1)
+            for i in range(4):
+                for u in range(2):
+                    o = u * 256 + (i % 2) * 128
+                    nc.tensor.transpose(
+                        xbank[e][i // 2][:, o : o + 128], words[:, i, base + u : base + 256 : 2], ident[:]
+                    )
+
+        def x_copy(e):
+            t = sb.tile([P, 2048], BF16, name="qin", tag="qin", bufs=3, align_bytes=64)
+            banks = xbank.pop(e)
+            for b in range(2):
+                nc.scalar.copy(
+                    out=t[:, b * 1024 : (b + 1) * 1024].bitcast(F32).rearrange("p (n u) -> p n u", u=2),
+                    in_=banks[b][:].rearrange("p (u n) -> p n u", u=2),
+                )
+            xin[e] = t
+
+        def x_quant(e):
+            tcx, g = divmod(e, 8)
+            xc[(g, tcx)] = sb.tile(
+                [P, 512], U32, name="xc%d_%d" % (g, tcx), tag="xc%d_%d" % (g, tcx), align_bytes=64
+            )
+            if g % 4 == 0:
+                xs[(g // 4, tcx)] = sb.tile(
+                    [P, 512], U8, name="xs%d_%d" % (g // 4, tcx), tag="xs%d_%d" % (g // 4, tcx), align_bytes=64
+                )
+            nc.vector.quantize_mx(
+                out=xc[(g, tcx)][:].bitcast(FP8X4), scales=xs[(g // 4, tcx)][4 * (g % 4) : P, :], in_=xin.pop(e)[:]
+            )
+
+        def y_load(s):
+            if s >= 32:
+                return
+            gg, tcx = divmod(s, 4)
+            t = sb.tile([P, 4, 512], BF16, name="yraw", tag="yraw", bufs=2)
+            nc.sync.dma_start(
+                out=t[:],
+                in_=yf[tcx * 512 : (tcx + 1) * 512, gg * 512 : (gg + 1) * 512].rearrange("(i p) c -> p i c", p=P),
+            )
+            yraw[s] = t
+
+        def y_sort(s):
+            t = sb.tile([P, 4, 512], BF16, name="ysrt", tag="ysrt", bufs=2)
+            nc.scalar.copy(
+                out=t[:].bitcast(F32).rearrange("p i (u m) -> p i u m", u=2),
+                in_=yraw.pop(s)[:].bitcast(F32).rearrange("p i (m u) -> p i u m", u=2),
+            )
+            ysrt[s] = t
+
+        def y_transpose(s):
+            words = ysrt.pop(s)[:].bitcast(F32)
+            b0 = ps.tile([P, 512], F32, name="yb", tag="yb", bufs=2)
+            b1 = ps.tile([P, 512], F32, name="yb", tag="yb", bufs=2)
+            ybank[s] = (b0, b1)
+            for i in range(4):
+                for u in range(2):
+                    o = u * 256 + (i % 2) * 128
+                    nc.tensor.transpose(
+                        ybank[s][i // 2][:, o : o + 128], words[:, i, u * 128 : (u + 1) * 128], ident[:]
+                    )
+
+        def new_acc(tag):
+            bufs = {"acc": 2, "yb": 2, "xb": 4}[tag]
+            return ps.tile([P, 512], F32, name=tag, tag=tag, bufs=bufs)
+
+        def next_acc():
+            n = counter["acc"]
+            counter["acc"] = n + 1
+            return new_acc(("acc", "xb", "xb", "acc", "xb", "xb")[n % 6])
+
+        def mm1(s, t, acc, g_lo, g_hi):
+            c, tcx = divmod(s, 4)
+            for g in range(g_lo, g_hi):
+                k = 4 * (g % 4)
+                nc.tensor.matmul_mx(
+                    out=acc[:],
+                    lhsT=wc[8 * c + g][:, t * 128 : (t + 1) * 128].bitcast(FP8X4),
+                    lhsT_scale=ws[(c, g // 4)][k:P, t * 128 : (t + 1) * 128],
+                    rhs=xc[(g, tcx)][:].bitcast(FP8X4),
+                    rhs_scale=xs[(g // 4, tcx)][k:P, :],
+                    start=(g == 0),
+                    stop=(g == 7),
+                )
+
+        def sigmoid(s, t, acc):
+            if t == 0:
+                sig[s] = sb.tile([P, 4, 512], F32, name="sig", tag="sig", bufs=2)
+            nc.scalar.activation(out=sig[s][:, t, :], in_=acc[:], func=ACT.Sigmoid)
+
+        def h_mul(s):
+            hb[s] = sb.tile([P, 2048], BF16, name="qin", tag="qin", bufs=3, align_bytes=64)
+            banks = ybank.pop(s)
+            for b in range(2):
+                nc.vector.tensor_tensor(
+                    out=hb[s][:, b * 1024 : (b + 1) * 1024].rearrange("p (n u e) -> p n u e", u=2, e=2),
+                    in0=sig[s][:, :, b * 256 : (b + 1) * 256].rearrange("p (u e) n -> p n u e", u=2),
+                    in1=banks[b][:].bitcast(BF16).rearrange("p (u n e) -> p n u e", u=2, e=2),
+                    op=ALU.mult,
+                )
+
+        def h_quant(s):
+            gg, tcx = divmod(s, 4)
+            if tcx == 0:
+                hc[gg] = sb.tile([P, 2048], U32, name="hc", tag="s8", bufs=8, align_bytes=64)
+            if gg % 4 == 0:
+                hs[(gg // 4, tcx)] = sb.tile(
+                    [P, 512], U8, name="hs%d_%d" % (gg // 4, tcx), tag="hs%d_%d" % (gg // 4, tcx), align_bytes=64
+                )
+            nc.vector.quantize_mx(
+                out=hc[gg][:, tcx * 512 : (tcx + 1) * 512].bitcast(FP8X4),
+                scales=hs[(gg // 4, tcx)][4 * (gg % 4) : P, :],
+                in_=hb.pop(s)[:],
+            )
+
+        def mm2(cc, i, acc):
+            for gg in range(8):
+                k = 4 * (gg % 4)
+                o = (i % 4) * 128
+                nc.tensor.matmul_mx(
+                    out=acc[:],
+                    lhsT=hc[gg][:, i * 128 : (i + 1) * 128].bitcast(FP8X4),
+                    lhsT_scale=hs[(gg // 4, i // 4)][k:P, o : o + 128],
+                    rhs=wc[8 * (8 + cc) + gg][:].bitcast(FP8X4),
+                    rhs_scale=ws[(8 + cc, gg // 4)][k:P, :],
+                    start=(gg == 0),
+                    stop=(gg == 7),
+                )
+
+        with tc.manual_schedule():
+            w_load(0)
+            x_load(0)
+            w_load(1)
+            w_load(2)
+            x_load(1)
+            acc0 = [new_acc("acc"), new_acc("acc"), new_acc("yb"), new_acc("yb")]
+            for q in range(8):
+                w_group(q)
+                if q >= 1 and q != 4:
+                    w_quant(q - 1)
+                if q <= 4:
+                    w_load(q + 3)
+                if q == 1:
+                    x_load(2)
+                if q >= 3:
+                    x_load(q)
+                if q == 6:
+                    y_load(0)
+                x_transpose(q)
+                x_copy(q)
+                if q >= 1 and q != 4:
+                    x_quant(q - 1)
+                if q == 3 or q == 7:
+                    w_quant(q)
+                    x_quant(q)
+                    for t in range(4):
+                        mm1(0, t, acc0[t], q - 3, q + 1)
+            y_load(1)
+            for t in range(4):
+                sigmoid(0, t, acc0[t])
+            pending = []
+            for st in range(4, 9):
+                for e in pending:
+                    x_quant(e)
+                pending = [2 * st, 2 * st + 1]
+                for e in pending:
+                    x_transpose(e)
+                    x_copy(e)
+                x_load(st + 4)
+                if st <= 6:
+                    w_load(st + 4)
+                if st == 5:
+                    y_sort(0)
+                    y_load(2)
+                if st == 6:
+                    y_transpose(0)
+
+            for s in range(1, 32):
+                c = s // 4
+                for t in range(4):
+                    k = (s % 4) * 4 + t
+                    if t == 3:
+                        y_transpose(s)
+                    acc = new_acc("acc") if c == 0 else next_acc()
+                    mm1(s, t, acc, 0, 8)
+                    sigmoid(s, t, acc)
+                    if t == 0:
+                        y_sort(s)
+                        y_load(s + 2)
+                    for e in pending:
+                        x_quant(e)
+                    pending = []
+                    if t == 0:
+                        h_mul(s - 1)
+                    if t == 1:
+                        h_quant(s - 1)
+                    w_background(c, k)
+                    st = k + 5
+                    if c == 0 and st <= 15:
+                        pending = [2 * st, 2 * st + 1]
+                        for e in pending:
+                            x_transpose(e)
+                            x_copy(e)
+                        x_load(st + 4)
+
+            ost = None
+            for cc in range(8):
+                for i in range(16):
+                    acc = next_acc()
+                    mm2(cc, i, acc)
+                    if i % 4 == 0:
+                        ost = sb.tile([P, 4, 512], F32, name="sig", tag="sig", bufs=2)
+                    if i % 2 == 0:
+                        nc.scalar.copy(out=ost[:, i % 4, :], in_=acc[:])
+                    else:
+                        nc.vector.tensor_copy(out=ost[:, i % 4, :], in_=acc[:])
+                    last = cc == 7 and i >= 12
+                    if last:
+                        nc.sync.dma_start(
+                            out=of[i * 128 : (i + 1) * 128, cc * 512 : (cc + 1) * 512], in_=ost[:, i % 4, :]
+                        )
+                    elif i % 4 == 3:
+                        nc.sync.dma_start(
+                            out=of[(i - 3) * 128 : (i + 1) * 128, cc * 512 : (cc + 1) * 512].rearrange(
+                                "(i p) c -> p i c", p=P
+                            ),
+                            in_=ost[:],
+                        )
+                    if cc == 0 and i == 0:
+                        h_mul(31)
+                    if cc == 0 and i == 1:
+                        h_quant(31)
+                    w_background(8 + cc, i)

@@ -63,20 +63,21 @@ def tile_multiheadattention_pb_l_kernel(tc, x, y_attn, w_gate, w_proj, out):
             )
             wraw[j] = t
 
-        def w_group(j):
+        def w_group(j, on_scalar=False):
             if j >= 128:
                 return
             g = sb.tile([P, 2048], BF16, name="wgrp", tag="wgrp", bufs=2, align_bytes=64)
             r = wraw.pop(j)
             if j < 64:
-                nc.vector.tensor_copy(
-                    out=g[:].rearrange("p (t m j) -> p t m j", t=4, j=4),
-                    in_=r[:].rearrange("p j (m t) -> p t m j", t=4),
-                )
+                dst = g[:].rearrange("p (t m j) -> p t m j", t=4, j=4)
+                src = r[:].rearrange("p j (m t) -> p t m j", t=4)
             else:
-                nc.vector.tensor_copy(
-                    out=g[:].rearrange("p (c j) -> p c j", j=4), in_=r[:].rearrange("p j c -> p c j")
-                )
+                dst = g[:].rearrange("p (c j) -> p c j", j=4)
+                src = r[:].rearrange("p j c -> p c j")
+            if on_scalar:
+                nc.scalar.copy(out=dst, in_=src)
+            else:
+                nc.vector.tensor_copy(out=dst, in_=src)
             wgrp[j] = g
 
         def w_quant(j):
@@ -114,7 +115,7 @@ def tile_multiheadattention_pb_l_kernel(tc, x, y_attn, w_gate, w_proj, out):
                 w_quant(j)
             j = plan.get((c, k, "g"))
             if j is not None:
-                w_group(j)
+                w_group(j, on_scalar=(1 <= c <= 7 and j % 8 in (1, 4, 6)))
                 w_load(j + 3)
 
         def x_load(st):
@@ -142,7 +143,7 @@ def tile_multiheadattention_pb_l_kernel(tc, x, y_attn, w_gate, w_proj, out):
                     )
 
         def x_copy(e):
-            t = sb.tile([P, 2048], BF16, name="qin", tag="qin", bufs=3, align_bytes=64)
+            t = sb.tile([P, 2048], BF16, name="qin", tag="qin", bufs=4, align_bytes=64)
             banks = xbank.pop(e)
             for b in range(2):
                 nc.scalar.copy(
@@ -168,41 +169,36 @@ def tile_multiheadattention_pb_l_kernel(tc, x, y_attn, w_gate, w_proj, out):
             if s >= 32:
                 return
             gg, tcx = divmod(s, 4)
-            t = sb.tile([P, 4, 512], BF16, name="yraw", tag="yraw", bufs=2)
-            nc.sync.dma_start(
-                out=t[:],
-                in_=yf[tcx * 512 : (tcx + 1) * 512, gg * 512 : (gg + 1) * 512].rearrange("(i p) c -> p i c", p=P),
-            )
+            t = sb.tile([P, 16, 128], BF16, name="yraw", tag="yraw", bufs=2)
+            for a in range(4):
+                col = gg * 512 + a * 128
+                nc.sync.dma_start(
+                    out=t[32 * a : 32 * a + 32, :, :],
+                    in_=yf[tcx * 512 : (tcx + 1) * 512, col : col + 128].rearrange("(g j) c -> j g c", j=32),
+                )
             yraw[s] = t
 
         def y_sort(s):
-            t = sb.tile([P, 4, 512], BF16, name="ysrt", tag="ysrt", bufs=2)
+            t = sb.tile([P, 2048], BF16, name="ysrt", tag="ysrt", bufs=1, align_bytes=64)
             nc.scalar.copy(
-                out=t[:].bitcast(F32).rearrange("p i (u m) -> p i u m", u=2),
-                in_=yraw.pop(s)[:].bitcast(F32).rearrange("p i (m u) -> p i u m", u=2),
+                out=t[:].bitcast(F32).rearrange("p (u g i) -> p u g i", u=2, g=16),
+                in_=yraw.pop(s)[:].bitcast(F32).rearrange("p g (i u) -> p u g i", u=2),
             )
             ysrt[s] = t
 
         def y_transpose(s):
-            words = ysrt.pop(s)[:].bitcast(F32)
-            b0 = ps.tile([P, 512], F32, name="yb", tag="yb", bufs=2)
-            b1 = ps.tile([P, 512], F32, name="yb", tag="yb", bufs=2)
-            ybank[s] = (b0, b1)
-            for i in range(4):
-                for u in range(2):
-                    o = u * 256 + (i % 2) * 128
-                    nc.tensor.transpose(
-                        ybank[s][i // 2][:, o : o + 128], words[:, i, u * 128 : (u + 1) * 128], ident[:]
-                    )
+            t = sb.tile([P, 2048], BF16, name="qin", tag="qin", bufs=4, align_bytes=64)
+            nc.vector.transpose(out=t[:].bitcast(F32), in_=ysrt.pop(s)[:].bitcast(F32))
+            ybank[s] = t
 
         def new_acc(tag):
-            bufs = {"acc": 2, "yb": 2, "xb": 4}[tag]
+            bufs = {"acc": 4, "xb": 4}[tag]
             return ps.tile([P, 512], F32, name=tag, tag=tag, bufs=bufs)
 
         def next_acc():
             n = counter["acc"]
             counter["acc"] = n + 1
-            return new_acc(("acc", "xb", "xb", "acc", "xb", "xb")[n % 6])
+            return new_acc(("acc", "xb")[n % 2])
 
         def mm1(s, t, acc, g_lo, g_hi):
             c, tcx = divmod(s, 4)
@@ -224,15 +220,13 @@ def tile_multiheadattention_pb_l_kernel(tc, x, y_attn, w_gate, w_proj, out):
             nc.scalar.activation(out=sig[s][:, t, :], in_=acc[:], func=ACT.Sigmoid)
 
         def h_mul(s):
-            hb[s] = sb.tile([P, 2048], BF16, name="qin", tag="qin", bufs=3, align_bytes=64)
-            banks = ybank.pop(s)
-            for b in range(2):
-                nc.vector.tensor_tensor(
-                    out=hb[s][:, b * 1024 : (b + 1) * 1024].rearrange("p (n u e) -> p n u e", u=2, e=2),
-                    in0=sig[s][:, :, b * 256 : (b + 1) * 256].rearrange("p (u e) n -> p n u e", u=2),
-                    in1=banks[b][:].bitcast(BF16).rearrange("p (u n e) -> p n u e", u=2, e=2),
-                    op=ALU.mult,
-                )
+            hb[s] = sb.tile([P, 2048], BF16, name="qin", tag="qin", bufs=4, align_bytes=64)
+            nc.vector.tensor_tensor(
+                out=hb[s][:].rearrange("p (n u e) -> p n u e", u=2, e=2),
+                in0=sig[s][:].rearrange("p (u e) n -> p n u e", u=2),
+                in1=ybank.pop(s)[:].rearrange("p (u n e) -> p n u e", u=2, e=2),
+                op=ALU.mult,
+            )
 
         def h_quant(s):
             gg, tcx = divmod(s, 4)
@@ -263,59 +257,82 @@ def tile_multiheadattention_pb_l_kernel(tc, x, y_attn, w_gate, w_proj, out):
                 )
 
         with tc.manual_schedule():
-            w_load(0)
-            x_load(0)
-            w_load(1)
-            w_load(2)
-            x_load(1)
-            acc0 = [new_acc("acc"), new_acc("acc"), new_acc("yb"), new_acc("yb")]
-            for q in range(8):
-                w_group(q)
-                if q >= 1 and q != 4:
-                    w_quant(q - 1)
-                if q <= 4:
-                    w_load(q + 3)
-                if q == 1:
-                    x_load(2)
-                if q >= 3:
-                    x_load(q)
-                if q == 6:
-                    y_load(0)
-                x_transpose(q)
-                x_copy(q)
-                if q >= 1 and q != 4:
-                    x_quant(q - 1)
-                if q == 3 or q == 7:
-                    w_quant(q)
-                    x_quant(q)
-                    for t in range(4):
-                        mm1(0, t, acc0[t], q - 3, q + 1)
-            y_load(1)
-            for t in range(4):
-                sigmoid(0, t, acc0[t])
-            pending = []
-            for st in range(4, 9):
-                for e in pending:
-                    x_quant(e)
-                pending = [2 * st, 2 * st + 1]
-                for e in pending:
+            def x_step(st):
+                for e in (2 * st, 2 * st + 1):
                     x_transpose(e)
                     x_copy(e)
-                x_load(st + 4)
-                if st <= 6:
-                    w_load(st + 4)
+
+            def x_step_quant(st):
+                x_quant(2 * st)
+                x_quant(2 * st + 1)
+
+            acc0 = [new_acc("acc"), new_acc("acc"), new_acc("acc"), new_acc("acc")]
+            x_load(0)
+            w_load(0)
+            w_load(1)
+            x_load(1)
+            w_load(2)
+            w_group(0)
+            w_load(3)
+            x_load(2)
+            x_step(0)
+            w_group(1)
+            w_load(4)
+            w_quant(0)
+            x_step_quant(0)
+            w_group(2)
+            w_load(5)
+            x_load(3)
+            x_step(1)
+            w_quant(1)
+            w_group(3)
+            w_load(6)
+            w_quant(2)
+            x_step_quant(1)
+            w_quant(3)
+            for t in range(4):
+                mm1(0, t, acc0[t], 0, 4)
+            w_group(4)
+            w_load(7)
+            for st in range(4, 9):
+                x_load(st)
+            x_step(2)
+            w_group(5)
+            w_quant(4)
+            w_group(6)
+            w_quant(5)
+            x_step(3)
+            w_group(7)
+            w_quant(6)
+            x_step_quant(2)
+            w_quant(7)
+            x_step_quant(3)
+            x_step(4)
+            y_load(0)
+            x_load(9)
+            for t in range(4):
+                mm1(0, t, acc0[t], 4, 8)
+            for t in range(4):
+                sigmoid(0, t, acc0[t])
+            for st in range(5, 9):
+                x_step_quant(st - 1)
+                x_step(st)
+                if st <= 7:
+                    w_load(st + 3)
+                x_load(st + 5)
                 if st == 5:
+                    y_load(1)
+                if st == 6:
                     y_sort(0)
                     y_load(2)
-                if st == 6:
+                if st == 7:
                     y_transpose(0)
+            pending = [16, 17]
 
             for s in range(1, 32):
                 c = s // 4
                 for t in range(4):
                     k = (s % 4) * 4 + t
-                    if t == 3:
-                        y_transpose(s)
                     acc = new_acc("acc") if c == 0 else next_acc()
                     mm1(s, t, acc, 0, 8)
                     sigmoid(s, t, acc)
@@ -329,6 +346,8 @@ def tile_multiheadattention_pb_l_kernel(tc, x, y_attn, w_gate, w_proj, out):
                         h_mul(s - 1)
                     if t == 1:
                         h_quant(s - 1)
+                    if t == 2:
+                        y_transpose(s)
                     w_background(c, k)
                     st = k + 5
                     if c == 0 and st <= 15:
@@ -336,7 +355,7 @@ def tile_multiheadattention_pb_l_kernel(tc, x, y_attn, w_gate, w_proj, out):
                         for e in pending:
                             x_transpose(e)
                             x_copy(e)
-                        x_load(st + 4)
+                        x_load(st + 5)
 
             ost = None
             for cc in range(8):

@@ -115,7 +115,7 @@ def tile_multiheadattention_pb_l_kernel(tc, x, y_attn, w_gate, w_proj, out):
                 w_quant(j)
             j = plan.get((c, k, "g"))
             if j is not None:
-                w_group(j, on_scalar=(1 <= c <= 7 and j % 8 in (1, 4, 6)))
+                w_group(j, on_scalar=(1 <= c <= 7 and j % 8 in (0, 2, 3, 5, 6)))
                 w_load(j + 3)
 
         def x_load(st):
@@ -165,10 +165,21 @@ def tile_multiheadattention_pb_l_kernel(tc, x, y_attn, w_gate, w_proj, out):
                 out=xc[(g, tcx)][:].bitcast(FP8X4), scales=xs[(g // 4, tcx)][4 * (g % 4) : P, :], in_=xin.pop(e)[:]
             )
 
+        def on_pe(s):
+            return s < 4 or s % 4 == 3
+
         def y_load(s):
             if s >= 32:
                 return
             gg, tcx = divmod(s, 4)
+            if on_pe(s):
+                t = sb.tile([P, 4, 512], BF16, name="yraw", tag="yraw", bufs=2)
+                nc.sync.dma_start(
+                    out=t[:],
+                    in_=yf[tcx * 512 : (tcx + 1) * 512, gg * 512 : (gg + 1) * 512].rearrange("(i p) c -> p i c", p=P),
+                )
+                yraw[s] = t
+                return
             t = sb.tile([P, 16, 128], BF16, name="yraw", tag="yraw", bufs=2)
             for a in range(4):
                 col = gg * 512 + a * 128
@@ -180,11 +191,29 @@ def tile_multiheadattention_pb_l_kernel(tc, x, y_attn, w_gate, w_proj, out):
 
         def y_sort(s):
             t = sb.tile([P, 2048], BF16, name="ysrt", tag="ysrt", bufs=1, align_bytes=64)
+            ysrt[s] = t
+            if on_pe(s):
+                nc.scalar.copy(
+                    out=t[:].bitcast(F32).rearrange("p (i u m) -> p i u m", i=4, u=2),
+                    in_=yraw.pop(s)[:].bitcast(F32).rearrange("p i (m u) -> p i u m", u=2),
+                )
+                return
             nc.scalar.copy(
                 out=t[:].bitcast(F32).rearrange("p (u g i) -> p u g i", u=2, g=16),
                 in_=yraw.pop(s)[:].bitcast(F32).rearrange("p g (i u) -> p u g i", u=2),
             )
             ysrt[s] = t
+
+        def y_transpose_pe(s):
+            words = ysrt.pop(s)[:].bitcast(F32)
+            b0 = ps.tile([P, 512], F32, name="yb", tag="yb", bufs=2)
+            b1 = ps.tile([P, 512], F32, name="yb", tag="yb", bufs=2)
+            ybank[s] = (b0, b1)
+            for i in range(4):
+                for u in range(2):
+                    o = u * 256 + (i % 2) * 128
+                    w0 = (2 * i + u) * 128
+                    nc.tensor.transpose(ybank[s][i // 2][:, o : o + 128], words[:, w0 : w0 + 128], ident[:])
 
         def y_transpose(s):
             t = sb.tile([P, 2048], BF16, name="qin", tag="qin", bufs=4, align_bytes=64)
@@ -192,13 +221,13 @@ def tile_multiheadattention_pb_l_kernel(tc, x, y_attn, w_gate, w_proj, out):
             ybank[s] = t
 
         def new_acc(tag):
-            bufs = {"acc": 4, "xb": 4}[tag]
+            bufs = {"acc": 2, "yb": 2, "xb": 4}[tag]
             return ps.tile([P, 512], F32, name=tag, tag=tag, bufs=bufs)
 
         def next_acc():
             n = counter["acc"]
             counter["acc"] = n + 1
-            return new_acc(("acc", "xb")[n % 2])
+            return new_acc(("acc", "xb", "xb")[n % 3])
 
         def mm1(s, t, acc, g_lo, g_hi):
             c, tcx = divmod(s, 4)
@@ -221,6 +250,16 @@ def tile_multiheadattention_pb_l_kernel(tc, x, y_attn, w_gate, w_proj, out):
 
         def h_mul(s):
             hb[s] = sb.tile([P, 2048], BF16, name="qin", tag="qin", bufs=4, align_bytes=64)
+            if on_pe(s):
+                banks = ybank.pop(s)
+                for b in range(2):
+                    nc.vector.tensor_tensor(
+                        out=hb[s][:, b * 1024 : (b + 1) * 1024].rearrange("p (n u e) -> p n u e", u=2, e=2),
+                        in0=sig[s][:, :, b * 256 : (b + 1) * 256].rearrange("p (u e) n -> p n u e", u=2),
+                        in1=banks[b][:].bitcast(BF16).rearrange("p (u n e) -> p n u e", u=2, e=2),
+                        op=ALU.mult,
+                    )
+                return
             nc.vector.tensor_tensor(
                 out=hb[s][:].rearrange("p (n u e) -> p n u e", u=2, e=2),
                 in0=sig[s][:].rearrange("p (u e) n -> p n u e", u=2),
@@ -266,7 +305,7 @@ def tile_multiheadattention_pb_l_kernel(tc, x, y_attn, w_gate, w_proj, out):
                 x_quant(2 * st)
                 x_quant(2 * st + 1)
 
-            acc0 = [new_acc("acc"), new_acc("acc"), new_acc("acc"), new_acc("acc")]
+            acc0 = [new_acc("acc"), new_acc("acc"), new_acc("yb"), new_acc("yb")]
             x_load(0)
             w_load(0)
             w_load(1)
@@ -288,8 +327,8 @@ def tile_multiheadattention_pb_l_kernel(tc, x, y_attn, w_gate, w_proj, out):
             w_group(3)
             w_load(6)
             w_quant(2)
-            x_step_quant(1)
             w_quant(3)
+            x_step_quant(1)
             for t in range(4):
                 mm1(0, t, acc0[t], 0, 4)
             w_group(4)
@@ -310,11 +349,9 @@ def tile_multiheadattention_pb_l_kernel(tc, x, y_attn, w_gate, w_proj, out):
             x_step(4)
             y_load(0)
             x_load(9)
-            for t in range(4):
-                mm1(0, t, acc0[t], 4, 8)
-            for t in range(4):
-                sigmoid(0, t, acc0[t])
             for st in range(5, 9):
+                mm1(0, st - 5, acc0[st - 5], 4, 8)
+                sigmoid(0, st - 5, acc0[st - 5])
                 x_step_quant(st - 1)
                 x_step(st)
                 if st <= 7:
@@ -325,14 +362,16 @@ def tile_multiheadattention_pb_l_kernel(tc, x, y_attn, w_gate, w_proj, out):
                 if st == 6:
                     y_sort(0)
                     y_load(2)
-                if st == 7:
-                    y_transpose(0)
+                if st == 8:
+                    y_transpose_pe(0)
             pending = [16, 17]
 
             for s in range(1, 32):
                 c = s // 4
                 for t in range(4):
                     k = (s % 4) * 4 + t
+                    if t == 3 and on_pe(s):
+                        y_transpose_pe(s)
                     acc = new_acc("acc") if c == 0 else next_acc()
                     mm1(s, t, acc, 0, 8)
                     sigmoid(s, t, acc)
@@ -346,7 +385,7 @@ def tile_multiheadattention_pb_l_kernel(tc, x, y_attn, w_gate, w_proj, out):
                         h_mul(s - 1)
                     if t == 1:
                         h_quant(s - 1)
-                    if t == 2:
+                    if t == 2 and not on_pe(s):
                         y_transpose(s)
                     w_background(c, k)
                     st = k + 5

@@ -115,7 +115,7 @@ def tile_multiheadattention_pb_l_kernel(tc, x, y_attn, w_gate, w_proj, out):
                 w_quant(j)
             j = plan.get((c, k, "g"))
             if j is not None:
-                w_group(j, on_scalar=(1 <= c <= 7 and j % 8 in (0, 2, 3, 5, 6)))
+                w_group(j, on_scalar=(1 <= c <= 7 and j % 8 in (1, 3, 5, 7)))
                 w_load(j + 3)
 
         def x_load(st):

from contextlib import ExitStack

import concourse.mybir as mybir
from concourse.masks import make_identity

FLOPS = 2 * 2 * 2048 * 4096 * 4096

F32 = mybir.dt.float32
BF16 = mybir.dt.bfloat16
U32 = mybir.dt.uint32
U8 = mybir.dt.uint8
FP8X4 = mybir.dt.float8_e4m3fn_x4
ACT = mybir.ActivationFunctionType
ALU = mybir.AluOpType

P = 128


def tile_multiheadattention_pb_l_kernel(tc, x, y_attn, w_gate, w_proj, out):
    nc = tc.nc
    xf = x.rearrange("b t c -> (b t) c")
    yf = y_attn.rearrange("b t h d -> (b t) (h d)")
    of = out.rearrange("b t c -> (b t) c")

    with ExitStack() as ctx:
        sb = ctx.enter_context(tc.tile_pool(name="sb", bufs=1))
        ps = ctx.enter_context(tc.psum_pool(name="ps", bufs=2))

        ident = sb.tile([P, P], F32, name="ident", tag="ident")
        make_identity(nc, ident[:])
        warm_in = sb.tile([P, 8], F32, name="warm_in", tag="warm_in")
        warm_out = sb.tile([P, 8], F32, name="warm_out", tag="warm_out")
        nc.vector.memset(warm_in[:], 0.0)
        nc.scalar.activation(out=warm_out[:], in_=warm_in[:], func=ACT.Sigmoid)

        wraw = {}
        wgrp = {}
        wc = {}
        ws = {}
        xraw = {}
        xbank = {}
        xin = {}
        xc = {}
        xs = {}
        yraw = {}
        ysrt = {}
        ybank = {}
        sig = {}
        hb = {}
        hc = {}
        hs = {}
        counter = {"acc": 0}

        def w_load(j):
            if j >= 128:
                return
            c, q = divmod(j, 8)
            src = w_gate if c < 8 else w_proj
            col = (c % 8) * 512
            t = sb.tile([P, 4, 512], BF16, name="wraw", tag="wraw", bufs=3)
            nc.sync.dma_start(
                out=t[:], in_=src[q * 512 : (q + 1) * 512, col : col + 512].rearrange("(p j) c -> p j c", j=4)
            )
            wraw[j] = t

        def w_group(j, on_scalar=False):
            if j >= 128:
                return
            g = sb.tile([P, 2048], BF16, name="wgrp", tag="wgrp", bufs=2, align_bytes=64)
            r = wraw.pop(j)
            if j < 64:
                dst = g[:].rearrange("p (t m j) -> p t m j", t=4, j=4)
                src = r[:].rearrange("p j (m t) -> p t m j", t=4)
            else:
                dst = g[:].rearrange("p (c j) -> p c j", j=4)
                src = r[:].rearrange("p j c -> p c j")
            if on_scalar:
                nc.scalar.copy(out=dst, in_=src)
            else:
                nc.vector.tensor_copy(out=dst, in_=src)
            wgrp[j] = g

        def w_quant(j):
            if j >= 128:
                return
            c, q = divmod(j, 8)
            wc[j] = sb.tile([P, 512], U32, name="wc%d" % q, tag="wc%d" % q, bufs=2, align_bytes=64)
            if q % 4 == 0:
                ws[(c, q // 4)] = sb.tile(
                    [P, 512], U8, name="ws%d" % (q // 4), tag="ws%d" % (q // 4), bufs=2, align_bytes=64
                )
            nc.vector.quantize_mx(
                out=wc[j][:].bitcast(FP8X4), scales=ws[(c, q // 4)][4 * (q % 4) : P, :], in_=wgrp.pop(j)[:]
            )

        plan = {}
        for c in range(16):
            for q in range(8):
                j = 8 * (c + 1) + q
                if c == 0:
                    kg = (4, 5, 7, 8, 10, 11, 13, 14)[q]
                    kq = kg + 1
                    plan[(0, kg, "g")] = j
                    plan[(0, kq, "q")] = j
                else:
                    if q == 0:
                        plan[(c - 1, 15, "g")] = j
                    else:
                        plan[(c, 2 * q - 1, "g")] = j
                    plan[(c, 2 * q, "q")] = j

        def w_background(c, k):
            j = plan.get((c, k, "q"))
            if j is not None:
                w_quant(j)
            j = plan.get((c, k, "g"))
            if j is not None:
                w_group(j, on_scalar=(1 <= c <= 7 and j % 8 in (1, 3, 5, 7)))
                w_load(j + 3)

        def x_load(st):
            if st >= 16:
                return
            tcx, gp = divmod(st, 4)
            t = sb.tile([P, 4, 1024], BF16, name="xraw", tag="s8", bufs=8, align_bytes=64)
            nc.sync.dma_start(
                out=t[:],
                in_=xf[tcx * 512 : (tcx + 1) * 512, gp * 1024 : (gp + 1) * 1024].rearrange("(i p) c -> p i c", p=P),
            )
            xraw[st] = t

        def x_transpose(e):
            words = xraw[e // 2][:].bitcast(F32)
            base = (e % 2) * 256
            b0 = ps.tile([P, 512], F32, name="xb", tag="xb", bufs=4)
            b1 = ps.tile([P, 512], F32, name="xb", tag="xb", bufs=4)
            xbank[e] = (b0, b1)
            for i in range(4):
                for u in range(2):
                    o = u * 256 + (i % 2) * 128
                    nc.tensor.transpose(
                        xbank[e][i // 2][:, o : o + 128], words[:, i, base + u : base + 256 : 2], ident[:]
                    )

        def x_copy(e):
            t = sb.tile([P, 2048], BF16, name="qin", tag="qin", bufs=4, align_bytes=64)
            banks = xbank.pop(e)
            for b in range(2):
                nc.scalar.copy(
                    out=t[:, b * 1024 : (b + 1) * 1024].bitcast(F32).rearrange("p (n u) -> p n u", u=2),
                    in_=banks[b][:].rearrange("p (u n) -> p n u", u=2),
                )
            xin[e] = t

        def x_quant(e):
            tcx, g = divmod(e, 8)
            xc[(g, tcx)] = sb.tile(
                [P, 512], U32, name="xc%d_%d" % (g, tcx), tag="xc%d_%d" % (g, tcx), align_bytes=64
            )
            if g % 4 == 0:
                xs[(g // 4, tcx)] = sb.tile(
                    [P, 512], U8, name="xs%d_%d" % (g // 4, tcx), tag="xs%d_%d" % (g // 4, tcx), align_bytes=64
                )
            nc.vector.quantize_mx(
                out=xc[(g, tcx)][:].bitcast(FP8X4), scales=xs[(g // 4, tcx)][4 * (g % 4) : P, :], in_=xin.pop(e)[:]
            )

        def on_pe(s):
            return s < 4 or s % 4 == 3

        def y_load(s):
            if s >= 32:
                return
            gg, tcx = divmod(s, 4)
            if on_pe(s):
                t = sb.tile([P, 4, 512], BF16, name="yraw", tag="yraw", bufs=2)
                nc.sync.dma_start(
                    out=t[:],
                    in_=yf[tcx * 512 : (tcx + 1) * 512, gg * 512 : (gg + 1) * 512].rearrange("(i p) c -> p i c", p=P),
                )
                yraw[s] = t
                return
            t = sb.tile([P, 16, 128], BF16, name="yraw", tag="yraw", bufs=2)
            for a in range(4):
                col = gg * 512 + a * 128
                nc.sync.dma_start(
                    out=t[32 * a : 32 * a + 32, :, :],
                    in_=yf[tcx * 512 : (tcx + 1) * 512, col : col + 128].rearrange("(g j) c -> j g c", j=32),
                )
            yraw[s] = t

        def y_sort(s):
            t = sb.tile([P, 2048], BF16, name="ysrt", tag="ysrt", bufs=1, align_bytes=64)
            ysrt[s] = t
            if on_pe(s):
                nc.scalar.copy(
                    out=t[:].bitcast(F32).rearrange("p (i u m) -> p i u m", i=4, u=2),
                    in_=yraw.pop(s)[:].bitcast(F32).rearrange("p i (m u) -> p i u m", u=2),
                )
                return
            nc.scalar.copy(
                out=t[:].bitcast(F32).rearrange("p (u g i) -> p u g i", u=2, g=16),
                in_=yraw.pop(s)[:].bitcast(F32).rearrange("p g (i u) -> p u g i", u=2),
            )
            ysrt[s] = t

        def y_transpose_pe(s):
            words = ysrt.pop(s)[:].bitcast(F32)
            b0 = ps.tile([P, 512], F32, name="yb", tag="yb", bufs=2)
            b1 = ps.tile([P, 512], F32, name="yb", tag="yb", bufs=2)
            ybank[s] = (b0, b1)
            for i in range(4):
                for u in range(2):
                    o = u * 256 + (i % 2) * 128
                    w0 = (2 * i + u) * 128
                    nc.tensor.transpose(ybank[s][i // 2][:, o : o + 128], words[:, w0 : w0 + 128], ident[:])

        def y_transpose(s):
            t = sb.tile([P, 2048], BF16, name="qin", tag="qin", bufs=4, align_bytes=64)
            nc.vector.transpose(out=t[:].bitcast(F32), in_=ysrt.pop(s)[:].bitcast(F32))
            ybank[s] = t

        def new_acc(tag):
            bufs = {"acc": 2, "yb": 2, "xb": 4}[tag]
            return ps.tile([P, 512], F32, name=tag, tag=tag, bufs=bufs)

        def next_acc():
            n = counter["acc"]
            counter["acc"] = n + 1
            return new_acc(("acc", "xb", "xb")[n % 3])

        def mm1(s, t, acc, g_lo, g_hi):
            c, tcx = divmod(s, 4)
            for g in range(g_lo, g_hi):
                k = 4 * (g % 4)
                nc.tensor.matmul_mx(
                    out=acc[:],
                    lhsT=wc[8 * c + g][:, t * 128 : (t + 1) * 128].bitcast(FP8X4),
                    lhsT_scale=ws[(c, g // 4)][k:P, t * 128 : (t + 1) * 128],
                    rhs=xc[(g, tcx)][:].bitcast(FP8X4),
                    rhs_scale=xs[(g // 4, tcx)][k:P, :],
                    start=(g == 0),
                    stop=(g == 7),
                )

        def sigmoid(s, t, acc):
            if t == 0:
                sig[s] = sb.tile([P, 4, 512], F32, name="sig", tag="sig", bufs=2)
            nc.scalar.activation(out=sig[s][:, t, :], in_=acc[:], func=ACT.Sigmoid)

        def h_mul(s):
            hb[s] = sb.tile([P, 2048], BF16, name="qin", tag="qin", bufs=4, align_bytes=64)
            if on_pe(s):
                banks = ybank.pop(s)
                for b in range(2):
                    nc.vector.tensor_tensor(
                        out=hb[s][:, b * 1024 : (b + 1) * 1024].rearrange("p (n u e) -> p n u e", u=2, e=2),
                        in0=sig[s][:, :, b * 256 : (b + 1) * 256].rearrange("p (u e) n -> p n u e", u=2),
                        in1=banks[b][:].bitcast(BF16).rearrange("p (u n e) -> p n u e", u=2, e=2),
                        op=ALU.mult,
                    )
                return
            nc.vector.tensor_tensor(
                out=hb[s][:].rearrange("p (n u e) -> p n u e", u=2, e=2),
                in0=sig[s][:].rearrange("p (u e) n -> p n u e", u=2),
                in1=ybank.pop(s)[:].rearrange("p (u n e) -> p n u e", u=2, e=2),
                op=ALU.mult,
            )

        def h_quant(s):
            gg, tcx = divmod(s, 4)
            if tcx == 0:
                hc[gg] = sb.tile([P, 2048], U32, name="hc", tag="s8", bufs=8, align_bytes=64)
            if gg % 4 == 0:
                hs[(gg // 4, tcx)] = sb.tile(
                    [P, 512], U8, name="hs%d_%d" % (gg // 4, tcx), tag="hs%d_%d" % (gg // 4, tcx), align_bytes=64
                )
            nc.vector.quantize_mx(
                out=hc[gg][:, tcx * 512 : (tcx + 1) * 512].bitcast(FP8X4),
                scales=hs[(gg // 4, tcx)][4 * (gg % 4) : P, :],
                in_=hb.pop(s)[:],
            )

        def mm2(cc, i, acc):
            for gg in range(8):
                k = 4 * (gg % 4)
                o = (i % 4) * 128
                nc.tensor.matmul_mx(
                    out=acc[:],
                    lhsT=hc[gg][:, i * 128 : (i + 1) * 128].bitcast(FP8X4),
                    lhsT_scale=hs[(gg // 4, i // 4)][k:P, o : o + 128],
                    rhs=wc[8 * (8 + cc) + gg][:].bitcast(FP8X4),
                    rhs_scale=ws[(8 + cc, gg // 4)][k:P, :],
                    start=(gg == 0),
                    stop=(gg == 7),
                )

        with tc.manual_schedule():
            def x_step(st):
                for e in (2 * st, 2 * st + 1):
                    x_transpose(e)
                    x_copy(e)

            def x_step_quant(st):
                x_quant(2 * st)
                x_quant(2 * st + 1)

            acc0 = [new_acc("acc"), new_acc("acc"), new_acc("yb"), new_acc("yb")]
            x_load(0)
            w_load(0)
            w_load(1)
            x_load(1)
            w_load(2)
            w_group(0)
            w_load(3)
            x_load(2)
            x_step(0)
            w_group(1)
            w_load(4)
            w_quant(0)
            x_step_quant(0)
            w_group(2)
            w_load(5)
            x_load(3)
            x_step(1)
            w_quant(1)
            w_group(3)
            w_load(6)
            w_quant(2)
            w_quant(3)
            x_step_quant(1)
            for t in range(4):
                mm1(0, t, acc0[t], 0, 4)
            w_group(4)
            w_load(7)
            for st in range(4, 9):
                x_load(st)
            x_step(2)
            w_group(5)
            w_quant(4)
            w_group(6)
            w_quant(5)
            x_step(3)
            w_group(7)
            w_quant(6)
            x_step_quant(2)
            w_quant(7)
            x_step_quant(3)
            x_step(4)
            y_load(0)
            x_load(9)
            for st in range(5, 9):
                mm1(0, st - 5, acc0[st - 5], 4, 8)
                sigmoid(0, st - 5, acc0[st - 5])
                x_step_quant(st - 1)
                x_step(st)
                if st <= 7:
                    w_load(st + 3)
                x_load(st + 5)
                if st == 5:
                    y_load(1)
                if st == 6:
                    y_sort(0)
                    y_load(2)
                if st == 8:
                    y_transpose_pe(0)
            pending = [16, 17]

            for s in range(1, 32):
                c = s // 4
                for t in range(4):
                    k = (s % 4) * 4 + t
                    if t == 3 and on_pe(s):
                        y_transpose_pe(s)
                    acc = new_acc("acc") if c == 0 else next_acc()
                    mm1(s, t, acc, 0, 8)
                    sigmoid(s, t, acc)
                    if t == 0:
                        y_sort(s)
                        y_load(s + 2)
                    for e in pending:
                        x_quant(e)
                    pending = []
                    if t == 0:
                        h_mul(s - 1)
                    if t == 1:
                        h_quant(s - 1)
                    if t == 2 and not on_pe(s):
                        y_transpose(s)
                    w_background(c, k)
                    st = k + 5
                    if c == 0 and st <= 15:
                        pending = [2 * st, 2 * st + 1]
                        for e in pending:
                            x_transpose(e)
                            x_copy(e)
                        x_load(st + 5)

            ost = None
            for cc in range(8):
                for i in range(16):
                    acc = next_acc()
                    mm2(cc, i, acc)
                    if i % 4 == 0:
                        ost = sb.tile([P, 4, 512], F32, name="sig", tag="sig", bufs=2)
                    if i % 2 == 0:
                        nc.scalar.copy(out=ost[:, i % 4, :], in_=acc[:])
                    else:
                        nc.vector.tensor_copy(out=ost[:, i % 4, :], in_=acc[:])
                    last = cc == 7 and i >= 12
                    if last:
                        nc.sync.dma_start(
                            out=of[i * 128 : (i + 1) * 128, cc * 512 : (cc + 1) * 512], in_=ost[:, i % 4, :]
                        )
                    elif i % 4 == 3:
                        nc.sync.dma_start(
                            out=of[(i - 3) * 128 : (i + 1) * 128, cc * 512 : (cc + 1) * 512].rearrange(
                                "(i p) c -> p i c", p=P
                            ),
                            in_=ost[:],
                        )
                    if cc == 0 and i == 0:
                        h_mul(31)
                    if cc == 0 and i == 1:
                        h_quant(31)
                    w_background(8 + cc, i)
